import numpy as np
import ml_dtypes


def mxq(x, axis, fmt="e4m3"):
    dtype, down = {"e4m3": (ml_dtypes.float8_e4m3fn, 7), "e5m2": (ml_dtypes.float8_e5m2, 14)}[fmt]
    v = np.moveaxis(np.asarray(x, np.float32).astype(ml_dtypes.bfloat16).astype(np.float64), axis, -1)
    blocks = v.reshape(v.shape[:-1] + (-1, 32))
    amax = np.abs(blocks).max(-1, keepdims=True)
    byte = np.maximum(np.where(amax > 0, np.frexp(amax)[1] - 1 + 127, 0) - down, 1)
    scale = np.exp2(byte - 127.0)
    codes = (blocks / scale).astype(np.float32).astype(dtype).astype(np.float64)
    return np.moveaxis((codes * scale).reshape(v.shape), -1, axis)


WIDE = False


def mx_kscale(k):
    if not WIDE:
        return np.ones(k)
    levels = np.array([10, -10, 5, -5, 0])
    if k % 512:
        return np.exp2(np.random.permutation(np.resize(levels, k // 32))).repeat(32)
    a = np.empty((k // 512, 16))
    for p in range(k // 512):
        a[p, :8] = np.random.permutation(np.resize(levels, 8))
        for g in range(8):
            far = levels[np.abs(levels - a[p, g]) >= 10]
            a[p, g + 8] = far[np.random.randint(len(far))]
    return np.exp2(a.ravel()).repeat(32)


BF16 = ml_dtypes.bfloat16


def bf(x):
    return np.asarray(x, np.float32).astype(BF16)


def f64(x):
    return np.asarray(x).astype(np.float64)


B, L, D, NH, F = 2, 2048, 512, 8, 4096
HD = D // NH
EPS = 1e-6
QUIET = 2e-3


def rmsnorm(x, w):
    return w * x * (1.0 / np.sqrt(np.mean(x * x, axis=-1, keepdims=True) + EPS))


def heads(y):
    return y.reshape(B, L, NH, HD).transpose(0, 2, 1, 3)


def setup_inputs():
    s = mx_kscale(D)
    amp = np.where(np.random.random((B, L, 1)) < 0.25, QUIET, 1.0)
    return {"x": bf(np.random.standard_normal((B, L, D)) * amp),
            "attn_norm_w": bf((1.0 + 0.1 * np.random.standard_normal(D)) * s),
            "W_q": bf(np.random.standard_normal((D, D)) / np.sqrt(D) / s),
            "W_k": bf(np.random.standard_normal((D, D)) / np.sqrt(D) / s),
            "W_v": bf(np.random.standard_normal((D, D)) * 2.0 / np.sqrt(D) / s)}


def reference(x, attn_norm_w, W_q, W_k, W_v):
    xq = mxq(rmsnorm(f64(x), f64(attn_norm_w)), 2, "e4m3")
    q = xq @ mxq(f64(W_q), 1, "e4m3").T
    k = xq @ mxq(f64(W_k), 1, "e4m3").T
    v = xq @ mxq(f64(W_v), 1, "e4m3").T
    return heads(q), heads(k), heads(v)

@@ -1,0 +1,249 @@
+from contextlib import ExitStack
+
+import concourse.mybir as mybir
+from concourse.masks import make_identity
+
+BF16 = mybir.dt.bfloat16
+F32 = mybir.dt.float32
+U32 = mybir.dt.uint32
+U8 = mybir.dt.uint8
+FP8X4 = mybir.dt.float8_e4m3fn_x4
+MULT = mybir.AluOpType.mult
+FUNC = mybir.ActivationFunctionType
+
+P = 128
+PACK = 4
+D = P * PACK
+BATCH = 2
+SEQ = 2048
+HEADS = 8
+HEAD_DIM = D // HEADS
+EPS = 1e-6
+PROJECTIONS = 3
+
+CHUNK_TILES = 8
+CHUNK_TOKENS = P * CHUNK_TILES
+CHUNKS_PER_BATCH = SEQ // CHUNK_TOKENS
+CHUNKS = BATCH * CHUNKS_PER_BATCH
+TOKEN_TILES = CHUNKS * CHUNK_TILES
+
+PAIR = 2
+PAIRS = TOKEN_TILES // PAIR
+CHUNK_PAIRS = CHUNK_TILES // PAIR
+STEP_BANKS = PAIR * PROJECTIONS
+QUANT_LEAD = 4
+STATS_LEAD = 6
+
+FLOPS = 2 * BATCH * SEQ * D * PROJECTIONS * D
+
+
+def tile_block_pa_t_kernel(tc, x, attn_norm_w, W_q, W_k, W_v, out_0, out_1, out_2):
+    nc = tc.nc
+    weights = (W_q, W_k, W_v)
+    outs = (out_0, out_1, out_2)
+    x_chunks = x.flatten_outer_dims().rearrange("(c p g) d -> c p g d", p=P, g=CHUNK_TILES)
+
+    with ExitStack() as stack:
+        keep = stack.enter_context(tc.tile_pool(name="keep", bufs=1))
+        junk_pool = stack.enter_context(tc.tile_pool(name="junk", bufs=2))
+        scaled_pool = stack.enter_context(tc.tile_pool(name="scaled", bufs=3))
+        normed_pool = stack.enter_context(tc.tile_pool(name="normed", bufs=2))
+        w_grouped_pool = stack.enter_context(tc.tile_pool(name="w_grouped", bufs=2))
+        unit_pool = stack.enter_context(tc.tile_pool(name="unit", bufs=6))
+        flip_pool = stack.enter_context(tc.psum_pool(name="flip", bufs=2))
+        acc_pool = stack.enter_context(tc.psum_pool(name="acc", bufs=STEP_BANKS))
+
+        x_sb = keep.tile([P, TOKEN_TILES, D], BF16)
+        w_sb = keep.tile([P, PROJECTIONS, PACK, D], BF16)
+        w_codes = keep.tile([P, PROJECTIONS, D], U32, align_bytes=64)
+        w_scales = keep.tile([P, PROJECTIONS, D], U8, align_bytes=64)
+        x_codes = keep.tile([P, TOKEN_TILES * P], U32, align_bytes=64)
+        x_scales = keep.tile([P, TOKEN_TILES * P], U8, align_bytes=64)
+        sum_sq = keep.tile([P, TOKEN_TILES], F32)
+        rms = keep.tile([P, TOKEN_TILES], F32)
+        inv_rms = keep.tile([P, TOKEN_TILES], F32)
+        ident_f32 = keep.tile([P, P], F32)
+        eps_col = keep.tile([P, 1], F32)
+        table_warm = keep.tile([P, 1], F32)
+        gain_col = keep.tile([P, PACK], BF16)
+
+        scaled = {}
+        flipped = {}
+        normed = {}
+        unit_now = {}
+
+        def load_x(pair):
+            chunk, part = divmod(pair, CHUNK_PAIRS)
+            nc.sync.dma_start(
+                out=x_sb[:, PAIR * pair : PAIR * (pair + 1), :],
+                in_=x_chunks[chunk, :, PAIR * part : PAIR * (part + 1), :],
+            )
+
+        def load_weight(which):
+            nc.sync.dma_start(
+                out=w_sb[:, which, :, :], in_=weights[which].rearrange("(fo p) k -> p fo k", p=P)
+            )
+
+        def prepare_weight(which):
+            w_grouped = w_grouped_pool.tile([P, D, PACK], BF16, align_bytes=64)
+            w_grouped_words = w_grouped[:].rearrange("p f t -> p (f t)").bitcast(F32)
+            for half in range(2):
+                w_flip = acc_pool.tile([P, 2, 2, P], F32, tag="acc")
+                for fo in range(2):
+                    w_words = w_sb[:, which, 2 * half + fo, :].bitcast(F32)
+                    for u in range(2):
+                        nc.tensor.transpose(w_flip[:, fo, u, :], w_words[:, u::2], ident_f32[:])
+                words = slice(half * 2 * P * 2, (half + 1) * 2 * P * 2)
+                dst = w_grouped_words[:, words].rearrange("p (fo f u) -> p fo f u", fo=2, u=2)
+                src = w_flip[:].rearrange("p fo u f -> p fo f u")
+                if half == 0:
+                    nc.vector.tensor_copy(out=dst, in_=src)
+                else:
+                    nc.scalar.copy(out=dst, in_=src)
+            nc.vector.quantize_mx(
+                out=w_codes[:, which, :].bitcast(FP8X4),
+                scales=w_scales[:, which, :],
+                in_=w_grouped[:].rearrange("p f t -> p (f t)"),
+            )
+
+        def sum_squares(pair):
+            for i in range(PAIR * pair, PAIR * (pair + 1)):
+                squares = junk_pool.tile([P, D], BF16)
+                nc.scalar.activation(
+                    out=squares[:], in_=x_sb[:, i, :], func=FUNC.Square, accum_out=sum_sq[:, i : i + 1]
+                )
+            cols = slice(PAIR * pair, PAIR * (pair + 1))
+            nc.scalar.activation(
+                out=rms[:, cols], in_=sum_sq[:, cols], func=FUNC.Sqrt, bias=eps_col[:], scale=1.0 / D
+            )
+
+        def scale_rows(pair):
+            cols = slice(PAIR * pair, PAIR * (pair + 1))
+            nc.vector.reciprocal(out=inv_rms[:, cols], in_=rms[:, cols])
+            x_over_rms = scaled_pool.tile([P, PAIR, PACK, P], F32)
+            for h in range(PAIR):
+                i = PAIR * pair + h
+                nc.gpsimd.tensor_scalar(
+                    out=x_over_rms[:, h, :, :],
+                    in0=x_sb[:, i, :].rearrange("l (q t) -> l t q", t=PACK),
+                    scalar1=inv_rms[:, i : i + 1],
+                    scalar2=1.0,
+                    op0=MULT,
+                    op1=MULT,
+                )
+            scaled[pair] = x_over_rms
+
+        def transpose_pair(pair):
+            banks = []
+            for h in range(PAIR):
+                x_flip = flip_pool.tile([P, PACK, P], F32, tag="flip")
+                for t in range(PACK):
+                    nc.tensor.transpose(x_flip[:, t, :], scaled[pair][:, h, t, :], ident_f32[:])
+                banks.append(x_flip)
+            flipped[pair] = banks
+
+        def apply_gain(pair):
+            xn = normed_pool.tile([P, PAIR, P, PACK], BF16, align_bytes=64)
+            for h in range(PAIR):
+                nc.vector.tensor_tensor(
+                    out=xn[:, h, :, :],
+                    in0=flipped[pair][h][:].rearrange("p t l -> p l t"),
+                    in1=gain_col[:].unsqueeze(1).to_broadcast([P, P, PACK]),
+                    op=MULT,
+                )
+            normed[pair] = xn
+
+        def quantise(pair):
+            cols = slice(pair * PAIR * P, (pair + 1) * PAIR * P)
+            nc.vector.quantize_mx(
+                out=x_codes[:, cols].bitcast(FP8X4),
+                scales=x_scales[:, cols],
+                in_=normed[pair][:].rearrange("p h l t -> p (h l t)"),
+            )
+
+        def project(bank):
+            chunk, rest = divmod(bank, PROJECTIONS * CHUNK_TILES)
+            which, g = divmod(rest, CHUNK_TILES)
+            if g == 0:
+                unit = unit_pool.tile([P, HEADS, CHUNK_TILES, HEAD_DIM], F32)
+                unit_now["tile"] = unit
+            unit = unit_now["tile"]
+            cols = slice((chunk * CHUNK_TILES + g) * P, (chunk * CHUNK_TILES + g + 1) * P)
+            acc = acc_pool.tile([P, D], F32, tag="acc")
+            nc.tensor.matmul_mx(
+                out=acc[:],
+                lhsT=x_codes[:, cols].bitcast(FP8X4),
+                lhsT_scale=x_scales[:, cols],
+                rhs=w_codes[:, which, :].bitcast(FP8X4),
+                rhs_scale=w_scales[:, which, :],
+                start=True,
+                stop=True,
+            )
+            by_head = acc[:].rearrange("p (n j) -> p n j", n=HEADS)
+            if bank % 2 == 0:
+                nc.scalar.copy(out=unit[:, :, g, :], in_=by_head)
+            else:
+                nc.vector.tensor_copy(out=unit[:, :, g, :], in_=by_head)
+            store_tiles = CHUNK_TILES // 2 if chunk == 0 else CHUNK_TILES
+            if (g + 1) % store_tiles == 0:
+                batch, part = divmod(chunk, CHUNKS_PER_BATCH)
+                rows = slice(part * CHUNK_TOKENS, (part + 1) * CHUNK_TOKENS)
+                tiles = slice(g + 1 - store_tiles, g + 1)
+                nc.sync.dma_start(
+                    out=outs[which][batch, :, rows, :].rearrange("n (p g) j -> p n g j", g=CHUNK_TILES)[
+                        :, :, tiles, :
+                    ],
+                    in_=unit[:, :, tiles, :],
+                )
+
+        stack.enter_context(tc.manual_schedule())
+
+        nc.vector.memset(eps_col[:], EPS)
+        make_identity(nc, ident_f32[:])
+        nc.scalar.dma_start(out=gain_col[:], in_=attn_norm_w.rearrange("(p t) -> p t", t=PACK))
+        nc.scalar.activation(out=table_warm[:], in_=eps_col[:], func=FUNC.Sqrt)
+        load_x(0)
+        load_x(1)
+        load_weight(0)
+        load_x(2)
+        load_x(3)
+        load_weight(1)
+        load_weight(2)
+        for pair in range(CHUNK_PAIRS, PAIRS):
+            load_x(pair)
+
+        for pair in range(STATS_LEAD - QUANT_LEAD):
+            sum_squares(pair)
+            scale_rows(pair)
+        prepare_weight(0)
+        for pair in range(QUANT_LEAD):
+            transpose_pair(pair)
+            apply_gain(pair)
+            sum_squares(pair + STATS_LEAD - QUANT_LEAD)
+            scale_rows(pair + STATS_LEAD - QUANT_LEAD)
+            quantise(pair)
+            if pair >= 1:
+                project(PAIR * (pair - 1))
+                project(PAIR * (pair - 1) + 1)
+        prepare_weight(1)
+        prepare_weight(2)
+
+        for first_bank in range(STEP_BANKS, PROJECTIONS * TOKEN_TILES, STEP_BANKS):
+            to_quantise = first_bank // STEP_BANKS - 1 + QUANT_LEAD
+            to_scale = first_bank // STEP_BANKS - 1 + STATS_LEAD
+            if to_quantise < PAIRS:
+                transpose_pair(to_quantise)
+            project(first_bank)
+            project(first_bank + 1)
+            if to_quantise < PAIRS:
+                apply_gain(to_quantise)
+            if to_scale < PAIRS:
+                sum_squares(to_scale)
+            project(first_bank + 2)
+            project(first_bank + 3)
+            if to_quantise < PAIRS:
+                quantise(to_quantise)
+            if to_scale < PAIRS:
+                scale_rows(to_scale)
+            project(first_bank + 4)
+            project(first_bank + 5)

@@ -21,18 +21,23 @@ HEAD_DIM = D // HEADS
 EPS = 1e-6
 PROJECTIONS = 3
 
-CHUNK_TILES = 8
-CHUNK_TOKENS = P * CHUNK_TILES
-CHUNKS_PER_BATCH = SEQ // CHUNK_TOKENS
-CHUNKS = BATCH * CHUNKS_PER_BATCH
-TOKEN_TILES = CHUNKS * CHUNK_TILES
+BATCH_TILES = SEQ // P
+HALF_TILES = BATCH_TILES // 2
+TOKEN_TILES = BATCH * BATCH_TILES
 
 PAIR = 2
 PAIRS = TOKEN_TILES // PAIR
-CHUNK_PAIRS = CHUNK_TILES // PAIR
-STEP_BANKS = PAIR * PROJECTIONS
-QUANT_LEAD = 4
-STATS_LEAD = 6
+HALF_PAIRS = HALF_TILES // PAIR
+BANKS = TOKEN_TILES * PROJECTIONS
+ACC_BANKS = 6
+
+QUANT_LEAD = 8
+PAIR_SPACING = 4
+SQUARES_AHEAD = 10
+SCALE_AHEAD = 8
+TRANSPOSE_AHEAD = 3
+GAIN_AHEAD = 2
+LAST_NORM_BANK = 68
 
 FLOPS = 2 * BATCH * SEQ * D * PROJECTIONS * D
 
@@ -41,7 +46,21 @@ def tile_block_pa_t_kernel(tc, x, attn_norm_w, W_q, W_k, W_v, out_0, out_1, out_
     nc = tc.nc
     weights = (W_q, W_k, W_v)
     outs = (out_0, out_1, out_2)
-    x_chunks = x.flatten_outer_dims().rearrange("(c p g) d -> c p g d", p=P, g=CHUNK_TILES)
+    x_by_partition = x.rearrange("b (p g) d -> b p g d", g=BATCH_TILES)
+
+    quarter = HALF_TILES // 2
+    stores = [(0, 0, 0, quarter), (0, 0, quarter, quarter), (0, 1, 0, HALF_TILES), (0, 2, 0, HALF_TILES)]
+    stores += [(0, which, HALF_TILES, HALF_TILES) for which in range(PROJECTIONS)]
+    stores += [(1, which, first, HALF_TILES) for first in (0, HALF_TILES) for which in (0, 1)]
+    stores += [(1, 2, 0, BATCH_TILES)]
+    banks = []
+    for store in stores:
+        batch, which, first, tiles = store
+        for g in range(first, first + tiles):
+            banks.append((batch, which, g, store if g == first + tiles - 1 else None))
+    first_bank = {}
+    for n, (batch, which, g, store) in enumerate(banks):
+        first_bank.setdefault((batch * BATCH_TILES + g) // PAIR, n)
 
     with ExitStack() as stack:
         keep = stack.enter_context(tc.tile_pool(name="keep", bufs=1))
@@ -49,12 +68,12 @@ def tile_block_pa_t_kernel(tc, x, attn_norm_w, W_q, W_k, W_v, out_0, out_1, out_
         scaled_pool = stack.enter_context(tc.tile_pool(name="scaled", bufs=3))
         normed_pool = stack.enter_context(tc.tile_pool(name="normed", bufs=2))
         w_grouped_pool = stack.enter_context(tc.tile_pool(name="w_grouped", bufs=2))
-        unit_pool = stack.enter_context(tc.tile_pool(name="unit", bufs=6))
+        unit_pool = stack.enter_context(tc.tile_pool(name="unit", bufs=4))
         flip_pool = stack.enter_context(tc.psum_pool(name="flip", bufs=2))
-        acc_pool = stack.enter_context(tc.psum_pool(name="acc", bufs=STEP_BANKS))
+        acc_pool = stack.enter_context(tc.psum_pool(name="acc", bufs=ACC_BANKS))
 
         x_sb = keep.tile([P, TOKEN_TILES, D], BF16)
-        w_sb = keep.tile([P, PROJECTIONS, PACK, D], BF16)
+        w_sb = keep.tile([P, PROJECTIONS, 2, 2, D], BF16)
         w_codes = keep.tile([P, PROJECTIONS, D], U32, align_bytes=64)
         w_scales = keep.tile([P, PROJECTIONS, D], U8, align_bytes=64)
         x_codes = keep.tile([P, TOKEN_TILES * P], U32, align_bytes=64)
@@ -67,43 +86,44 @@ def tile_block_pa_t_kernel(tc, x, attn_norm_w, W_q, W_k, W_v, out_0, out_1, out_
         table_warm = keep.tile([P, 1], F32)
         gain_col = keep.tile([P, PACK], BF16)
 
+        grouped = {}
         scaled = {}
         flipped = {}
         normed = {}
-        unit_now = {}
+        units = {}
 
-        def load_x(pair):
-            chunk, part = divmod(pair, CHUNK_PAIRS)
+        def load_x(batch, first, tiles):
+            start = batch * BATCH_TILES + first
             nc.sync.dma_start(
-                out=x_sb[:, PAIR * pair : PAIR * (pair + 1), :],
-                in_=x_chunks[chunk, :, PAIR * part : PAIR * (part + 1), :],
+                out=x_sb[:, start : start + tiles, :], in_=x_by_partition[batch, :, first : first + tiles, :]
             )
 
         def load_weight(which):
             nc.sync.dma_start(
-                out=w_sb[:, which, :, :], in_=weights[which].rearrange("(fo p) k -> p fo k", p=P)
+                out=w_sb[:, which, :, :, :],
+                in_=weights[which].rearrange("(h p i) k -> p h i k", h=2, i=2),
             )
 
-        def prepare_weight(which):
+        def transpose_weight(which, copy):
             w_grouped = w_grouped_pool.tile([P, D, PACK], BF16, align_bytes=64)
+            grouped[which] = w_grouped
             w_grouped_words = w_grouped[:].rearrange("p f t -> p (f t)").bitcast(F32)
             for half in range(2):
                 w_flip = acc_pool.tile([P, 2, 2, P], F32, tag="acc")
-                for fo in range(2):
-                    w_words = w_sb[:, which, 2 * half + fo, :].bitcast(F32)
+                for i in range(2):
+                    w_words = w_sb[:, which, half, i, :].bitcast(F32)
                     for u in range(2):
-                        nc.tensor.transpose(w_flip[:, fo, u, :], w_words[:, u::2], ident_f32[:])
+                        nc.tensor.transpose(w_flip[:, i, u, :], w_words[:, u::2], ident_f32[:])
                 words = slice(half * 2 * P * 2, (half + 1) * 2 * P * 2)
-                dst = w_grouped_words[:, words].rearrange("p (fo f u) -> p fo f u", fo=2, u=2)
-                src = w_flip[:].rearrange("p fo u f -> p fo f u")
-                if half == 0:
-                    nc.vector.tensor_copy(out=dst, in_=src)
-                else:
-                    nc.scalar.copy(out=dst, in_=src)
+                dst = w_grouped_words[:, words].rearrange("p (f i u) -> p f i u", i=2, u=2)
+                src = w_flip[:].rearrange("p i u f -> p f i u")
+                copy(out=dst, in_=src)
+
+        def quantise_weight(which):
             nc.vector.quantize_mx(
                 out=w_codes[:, which, :].bitcast(FP8X4),
                 scales=w_scales[:, which, :],
-                in_=w_grouped[:].rearrange("p f t -> p (f t)"),
+                in_=grouped[which][:].rearrange("p f t -> p (f t)"),
             )
 
         def sum_squares(pair):
@@ -134,13 +154,13 @@ def tile_block_pa_t_kernel(tc, x, attn_norm_w, W_q, W_k, W_v, out_0, out_1, out_
             scaled[pair] = x_over_rms
 
         def transpose_pair(pair):
-            banks = []
+            x_flips = []
             for h in range(PAIR):
                 x_flip = flip_pool.tile([P, PACK, P], F32, tag="flip")
                 for t in range(PACK):
                     nc.tensor.transpose(x_flip[:, t, :], scaled[pair][:, h, t, :], ident_f32[:])
-                banks.append(x_flip)
-            flipped[pair] = banks
+                x_flips.append(x_flip)
+            flipped[pair] = x_flips
 
         def apply_gain(pair):
             xn = normed_pool.tile([P, PAIR, P, PACK], BF16, align_bytes=64)
@@ -162,13 +182,12 @@ def tile_block_pa_t_kernel(tc, x, attn_norm_w, W_q, W_k, W_v, out_0, out_1, out_
             )
 
         def project(bank):
-            chunk, rest = divmod(bank, PROJECTIONS * CHUNK_TILES)
-            which, g = divmod(rest, CHUNK_TILES)
-            if g == 0:
-                unit = unit_pool.tile([P, HEADS, CHUNK_TILES, HEAD_DIM], F32)
-                unit_now["tile"] = unit
-            unit = unit_now["tile"]
-            cols = slice((chunk * CHUNK_TILES + g) * P, (chunk * CHUNK_TILES + g + 1) * P)
+            batch, which, g, store = banks[bank]
+            if (batch, which) not in units:
+                new_unit = unit_pool.tile([P, HEADS, BATCH_TILES, HEAD_DIM], F32)
+                units[(batch, which)] = new_unit
+            unit = units[(batch, which)]
+            cols = slice((batch * BATCH_TILES + g) * P, (batch * BATCH_TILES + g + 1) * P)
             acc = acc_pool.tile([P, D], F32, tag="acc")
             nc.tensor.matmul_mx(
                 out=acc[:],
@@ -180,21 +199,14 @@ def tile_block_pa_t_kernel(tc, x, attn_norm_w, W_q, W_k, W_v, out_0, out_1, out_
                 stop=True,
             )
             by_head = acc[:].rearrange("p (n j) -> p n j", n=HEADS)
-            if bank % 2 == 0:
+            if bank < HALF_TILES - 1 or (bank % 7 in (0, 2, 4, 5) if bank < LAST_NORM_BANK else bank % 2 == 0):
                 nc.scalar.copy(out=unit[:, :, g, :], in_=by_head)
             else:
                 nc.vector.tensor_copy(out=unit[:, :, g, :], in_=by_head)
-            store_tiles = CHUNK_TILES // 2 if chunk == 0 else CHUNK_TILES
-            if (g + 1) % store_tiles == 0:
-                batch, part = divmod(chunk, CHUNKS_PER_BATCH)
-                rows = slice(part * CHUNK_TOKENS, (part + 1) * CHUNK_TOKENS)
-                tiles = slice(g + 1 - store_tiles, g + 1)
-                nc.sync.dma_start(
-                    out=outs[which][batch, :, rows, :].rearrange("n (p g) j -> p n g j", g=CHUNK_TILES)[
-                        :, :, tiles, :
-                    ],
-                    in_=unit[:, :, tiles, :],
-                )
+            if store is not None:
+                tiles = slice(store[2], store[2] + store[3])
+                by_partition = outs[which][batch, :, :, :].rearrange("n (p g) j -> p n g j", g=BATCH_TILES)
+                nc.sync.dma_start(out=by_partition[:, :, tiles, :], in_=unit[:, :, tiles, :])
 
         stack.enter_context(tc.manual_schedule())
 
@@ -202,48 +214,63 @@ def tile_block_pa_t_kernel(tc, x, attn_norm_w, W_q, W_k, W_v, out_0, out_1, out_
         make_identity(nc, ident_f32[:])
         nc.scalar.dma_start(out=gain_col[:], in_=attn_norm_w.rearrange("(p t) -> p t", t=PACK))
         nc.scalar.activation(out=table_warm[:], in_=eps_col[:], func=FUNC.Sqrt)
-        load_x(0)
-        load_x(1)
+        load_x(0, 0, PAIR)
         load_weight(0)
-        load_x(2)
-        load_x(3)
+        for pair in range(1, QUANT_LEAD):
+            load_x(0, PAIR * pair, PAIR)
         load_weight(1)
+        load_x(0, HALF_TILES, HALF_TILES)
         load_weight(2)
-        for pair in range(CHUNK_PAIRS, PAIRS):
-            load_x(pair)
+        load_x(1, 0, BATCH_TILES)
 
-        for pair in range(STATS_LEAD - QUANT_LEAD):
-            sum_squares(pair)
-            scale_rows(pair)
-        prepare_weight(0)
-        for pair in range(QUANT_LEAD):
-            transpose_pair(pair)
-            apply_gain(pair)
-            sum_squares(pair + STATS_LEAD - QUANT_LEAD)
-            scale_rows(pair + STATS_LEAD - QUANT_LEAD)
-            quantise(pair)
-            if pair >= 1:
-                project(PAIR * (pair - 1))
-                project(PAIR * (pair - 1) + 1)
-        prepare_weight(1)
-        prepare_weight(2)
+        sum_squares(0)
+        scale_rows(0)
+        transpose_weight(0, nc.vector.tensor_copy)
+        sum_squares(1)
+        scale_rows(1)
+        transpose_pair(0)
+        sum_squares(2)
+        apply_gain(0)
+        scale_rows(2)
+        quantise_weight(0)
+        sum_squares(3)
+        transpose_pair(1)
+        quantise(0)
+        apply_gain(1)
+        scale_rows(3)
+        transpose_weight(1, nc.scalar.copy)
+        project(0)
+        project(1)
+        transpose_pair(2)
+        quantise(1)
+        apply_gain(2)
+        project(2)
+        project(3)
+        transpose_pair(3)
+        quantise(2)
+        apply_gain(3)
+        project(4)
+        project(5)
+        quantise(3)
+        quantise_weight(1)
 
-        for first_bank in range(STEP_BANKS, PROJECTIONS * TOKEN_TILES, STEP_BANKS):
-            to_quantise = first_bank // STEP_BANKS - 1 + QUANT_LEAD
-            to_scale = first_bank // STEP_BANKS - 1 + STATS_LEAD
-            if to_quantise < PAIRS:
-                transpose_pair(to_quantise)
-            project(first_bank)
-            project(first_bank + 1)
-            if to_quantise < PAIRS:
-                apply_gain(to_quantise)
-            if to_scale < PAIRS:
-                sum_squares(to_scale)
-            project(first_bank + 2)
-            project(first_bank + 3)
-            if to_quantise < PAIRS:
-                quantise(to_quantise)
-            if to_scale < PAIRS:
-                scale_rows(to_scale)
-            project(first_bank + 4)
-            project(first_bank + 5)
+        due = {}
+        for pair in range(HALF_PAIRS, PAIRS):
+            quant_bank = first_bank[pair - pair % HALF_PAIRS] - QUANT_LEAD + PAIR_SPACING * (pair % HALF_PAIRS)
+            for ahead, stage in (
+                (0, quantise),
+                (GAIN_AHEAD, apply_gain),
+                (TRANSPOSE_AHEAD, transpose_pair),
+                (SCALE_AHEAD, scale_rows),
+                (SQUARES_AHEAD, sum_squares),
+            ):
+                due.setdefault(quant_bank - ahead, []).append((stage, pair))
+        w_v_bank = 10
+        for bank in range(6, BANKS):
+            if bank == w_v_bank:
+                transpose_weight(2, nc.vector.tensor_copy)
+            if bank == w_v_bank + 2:
+                quantise_weight(2)
+            for stage, pair in due.get(bank, []):
+                stage(pair)
+            project(bank)

@@ -216,7 +216,7 @@ def tile_block_pa_t_kernel(tc, x, attn_norm_w, W_q, W_k, W_v, out_0, out_1, out_
         nc.scalar.activation(out=table_warm[:], in_=eps_col[:], func=FUNC.Sqrt)
         load_x(0, 0, PAIR)
         load_weight(0)
-        for pair in range(1, QUANT_LEAD):
+        for pair in range(1, HALF_PAIRS):
             load_x(0, PAIR * pair, PAIR)
         load_weight(1)
         load_x(0, HALF_TILES, HALF_TILES)

@@ -84,6 +84,7 @@ def tile_block_pa_t_kernel(tc, x, attn_norm_w, W_q, W_k, W_v, out_0, out_1, out_
         ident_f32 = keep.tile([P, P], F32)
         eps_col = keep.tile([P, 1], F32)
         table_warm = keep.tile([P, 1], F32)
+        zeros = keep.tile([P, D], BF16)
         gain_col = keep.tile([P, PACK], BF16)
 
         grouped = {}
@@ -91,6 +92,11 @@ def tile_block_pa_t_kernel(tc, x, attn_norm_w, W_q, W_k, W_v, out_0, out_1, out_
         flipped = {}
         normed = {}
         units = {}
+
+        def keep_warm(count):
+            nothing = acc_pool.tile([P, D], F32, tag="acc")
+            for i in range(count):
+                nc.tensor.matmul(nothing[:], lhsT=zeros[:, 0:P], rhs=zeros[:], start=True, stop=True)
 
         def load_x(batch, first, tiles):
             start = batch * BATCH_TILES + first
@@ -211,6 +217,7 @@ def tile_block_pa_t_kernel(tc, x, attn_norm_w, W_q, W_k, W_v, out_0, out_1, out_
         stack.enter_context(tc.manual_schedule())
 
         nc.vector.memset(eps_col[:], EPS)
+        nc.vector.memset(zeros[:], 0.0)
         make_identity(nc, ident_f32[:])
         nc.scalar.dma_start(out=gain_col[:], in_=attn_norm_w.rearrange("(p t) -> p t", t=PACK))
         nc.scalar.activation(out=table_warm[:], in_=eps_col[:], func=FUNC.Sqrt)
@@ -223,18 +230,22 @@ def tile_block_pa_t_kernel(tc, x, attn_norm_w, W_q, W_k, W_v, out_0, out_1, out_
         load_weight(2)
         load_x(1, 0, BATCH_TILES)
 
+        keep_warm(8)
         sum_squares(0)
         scale_rows(0)
         transpose_weight(0, nc.vector.tensor_copy)
         sum_squares(1)
         scale_rows(1)
+        keep_warm(2)
         transpose_pair(0)
+        keep_warm(2)
         sum_squares(2)
         apply_gain(0)
         scale_rows(2)
         quantise_weight(0)
         sum_squares(3)
         transpose_pair(1)
+        keep_warm(2)
         quantise(0)
         apply_gain(1)
         scale_rows(3)
@@ -242,11 +253,13 @@ def tile_block_pa_t_kernel(tc, x, attn_norm_w, W_q, W_k, W_v, out_0, out_1, out_
         project(0)
         project(1)
         transpose_pair(2)
+        keep_warm(1)
         quantise(1)
         apply_gain(2)
         project(2)
         project(3)
         transpose_pair(3)
+        keep_warm(1)
         quantise(2)
         apply_gain(3)
         project(4)

@@ -29,15 +29,16 @@ PAIR = 2
 PAIRS = TOKEN_TILES // PAIR
 HALF_PAIRS = HALF_TILES // PAIR
 BANKS = TOKEN_TILES * PROJECTIONS
-ACC_BANKS = 6
+ACC_BANKS = 5
 
 QUANT_LEAD = 8
 PAIR_SPACING = 4
-SQUARES_AHEAD = 10
-SCALE_AHEAD = 8
+SQUARES_AHEAD = 12
+SCALE_AHEAD = 10
 TRANSPOSE_AHEAD = 3
 GAIN_AHEAD = 2
 LAST_NORM_BANK = 68
+W_V_BANK = 10
 
 FLOPS = 2 * BATCH * SEQ * D * PROJECTIONS * D
 
@@ -69,7 +70,7 @@ def tile_block_pa_t_kernel(tc, x, attn_norm_w, W_q, W_k, W_v, out_0, out_1, out_
         normed_pool = stack.enter_context(tc.tile_pool(name="normed", bufs=2))
         w_grouped_pool = stack.enter_context(tc.tile_pool(name="w_grouped", bufs=2))
         unit_pool = stack.enter_context(tc.tile_pool(name="unit", bufs=4))
-        flip_pool = stack.enter_context(tc.psum_pool(name="flip", bufs=2))
+        flip_pool = stack.enter_context(tc.psum_pool(name="flip", bufs=3))
         acc_pool = stack.enter_context(tc.psum_pool(name="acc", bufs=ACC_BANKS))
 
         x_sb = keep.tile([P, TOKEN_TILES, D], BF16)
@@ -205,7 +206,7 @@ def tile_block_pa_t_kernel(tc, x, attn_norm_w, W_q, W_k, W_v, out_0, out_1, out_
                 stop=True,
             )
             by_head = acc[:].rearrange("p (n j) -> p n j", n=HEADS)
-            if bank < HALF_TILES - 1 or (bank % 7 in (0, 2, 4, 5) if bank < LAST_NORM_BANK else bank % 2 == 0):
+            if bank < 6 or bank >= HALF_TILES and (bank % 7 in (0, 2, 4, 5) if bank < LAST_NORM_BANK else bank % 2 == 0):
                 nc.scalar.copy(out=unit[:, :, g, :], in_=by_head)
             else:
                 nc.vector.tensor_copy(out=unit[:, :, g, :], in_=by_head)
@@ -213,6 +214,27 @@ def tile_block_pa_t_kernel(tc, x, attn_norm_w, W_q, W_k, W_v, out_0, out_1, out_
                 tiles = slice(store[2], store[2] + store[3])
                 by_partition = outs[which][batch, :, :, :].rearrange("n (p g) j -> p n g j", g=BATCH_TILES)
                 nc.sync.dma_start(out=by_partition[:, :, tiles, :], in_=unit[:, :, tiles, :])
+
+        due = {}
+        for pair in range(HALF_PAIRS, PAIRS):
+            quant_bank = first_bank[pair - pair % HALF_PAIRS] - QUANT_LEAD + PAIR_SPACING * (pair % HALF_PAIRS)
+            for ahead, stage in (
+                (0, quantise),
+                (GAIN_AHEAD, apply_gain),
+                (TRANSPOSE_AHEAD, transpose_pair),
+                (SCALE_AHEAD, scale_rows),
+                (SQUARES_AHEAD, sum_squares),
+            ):
+                due.setdefault(quant_bank - ahead, []).append((stage, pair))
+
+        def results(bank):
+            if bank == W_V_BANK:
+                transpose_weight(2, nc.vector.tensor_copy)
+            if bank == W_V_BANK + 2:
+                quantise_weight(2)
+            for stage, pair in due.get(bank, []):
+                stage(pair)
+            project(bank)
 
         stack.enter_context(tc.manual_schedule())
 
@@ -250,40 +272,22 @@ def tile_block_pa_t_kernel(tc, x, attn_norm_w, W_q, W_k, W_v, out_0, out_1, out_
         apply_gain(1)
         scale_rows(3)
         transpose_weight(1, nc.scalar.copy)
-        project(0)
-        project(1)
+        results(0)
+        results(1)
         transpose_pair(2)
         keep_warm(1)
         quantise(1)
         apply_gain(2)
-        project(2)
-        project(3)
+        results(2)
+        results(3)
         transpose_pair(3)
         keep_warm(1)
         quantise(2)
         apply_gain(3)
-        project(4)
-        project(5)
+        results(4)
+        results(5)
         quantise(3)
         quantise_weight(1)
 
-        due = {}
-        for pair in range(HALF_PAIRS, PAIRS):
-            quant_bank = first_bank[pair - pair % HALF_PAIRS] - QUANT_LEAD + PAIR_SPACING * (pair % HALF_PAIRS)
-            for ahead, stage in (
-                (0, quantise),
-                (GAIN_AHEAD, apply_gain),
-                (TRANSPOSE_AHEAD, transpose_pair),
-                (SCALE_AHEAD, scale_rows),
-                (SQUARES_AHEAD, sum_squares),
-            ):
-                due.setdefault(quant_bank - ahead, []).append((stage, pair))
-        w_v_bank = 10
         for bank in range(6, BANKS):
-            if bank == w_v_bank:
-                transpose_weight(2, nc.vector.tensor_copy)
-            if bank == w_v_bank + 2:
-                quantise_weight(2)
-            for stage, pair in due.get(bank, []):
-                stage(pair)
-            project(bank)
+            results(bank)

@@ -34,7 +34,7 @@ ACC_BANKS = 5
 QUANT_LEAD = 8
 PAIR_SPACING = 4
 SQUARES_AHEAD = 12
-SCALE_AHEAD = 10
+SCALE_AHEAD = 8
 TRANSPOSE_AHEAD = 3
 GAIN_AHEAD = 2
 LAST_NORM_BANK = 68
@@ -206,7 +206,7 @@ def tile_block_pa_t_kernel(tc, x, attn_norm_w, W_q, W_k, W_v, out_0, out_1, out_
                 stop=True,
             )
             by_head = acc[:].rearrange("p (n j) -> p n j", n=HEADS)
-            if bank < 6 or bank >= HALF_TILES and (bank % 7 in (0, 2, 4, 5) if bank < LAST_NORM_BANK else bank % 2 == 0):
+            if bank < 6 or bank >= HALF_TILES and (bank % 5 in (0, 2, 3) if bank < LAST_NORM_BANK else bank % 2 == 0):
                 nc.scalar.copy(out=unit[:, :, g, :], in_=by_head)
             else:
                 nc.vector.tensor_copy(out=unit[:, :, g, :], in_=by_head)
@@ -264,14 +264,14 @@ def tile_block_pa_t_kernel(tc, x, attn_norm_w, W_q, W_k, W_v, out_0, out_1, out_
         sum_squares(2)
         apply_gain(0)
         scale_rows(2)
-        quantise_weight(0)
         sum_squares(3)
+        transpose_weight(1, nc.scalar.copy)
+        quantise_weight(0)
         transpose_pair(1)
         keep_warm(2)
         quantise(0)
         apply_gain(1)
         scale_rows(3)
-        transpose_weight(1, nc.scalar.copy)
         results(0)
         results(1)
         transpose_pair(2)

@@ -31,14 +31,14 @@ HALF_PAIRS = HALF_TILES // PAIR
 BANKS = TOKEN_TILES * PROJECTIONS
 ACC_BANKS = 5
 
-QUANT_LEAD = 8
+QUANT_LEAD = (8, 7)
 PAIR_SPACING = 4
 SQUARES_AHEAD = 12
 SCALE_AHEAD = 8
 TRANSPOSE_AHEAD = 3
 GAIN_AHEAD = 2
 LAST_NORM_BANK = 68
-W_V_BANK = 10
+W_V_BANK = 6
 
 FLOPS = 2 * BATCH * SEQ * D * PROJECTIONS * D
 
@@ -50,7 +50,7 @@ def tile_block_pa_t_kernel(tc, x, attn_norm_w, W_q, W_k, W_v, out_0, out_1, out_
     x_by_partition = x.rearrange("b (p g) d -> b p g d", g=BATCH_TILES)
 
     quarter = HALF_TILES // 2
-    stores = [(0, 0, 0, quarter), (0, 0, quarter, quarter), (0, 1, 0, HALF_TILES), (0, 2, 0, HALF_TILES)]
+    stores = [(0, which, first, quarter) for which in (0, 1) for first in (0, quarter)] + [(0, 2, 0, HALF_TILES)]
     stores += [(0, which, HALF_TILES, HALF_TILES) for which in range(PROJECTIONS)]
     stores += [(1, which, first, HALF_TILES) for first in (0, HALF_TILES) for which in (0, 1)]
     stores += [(1, 2, 0, BATCH_TILES)]
@@ -111,7 +111,7 @@ def tile_block_pa_t_kernel(tc, x, attn_norm_w, W_q, W_k, W_v, out_0, out_1, out_
                 in_=weights[which].rearrange("(h p i) k -> p h i k", h=2, i=2),
             )
 
-        def transpose_weight(which, copy):
+        def transpose_weight(which, copies):
             w_grouped = w_grouped_pool.tile([P, D, PACK], BF16, align_bytes=64)
             grouped[which] = w_grouped
             w_grouped_words = w_grouped[:].rearrange("p f t -> p (f t)").bitcast(F32)
@@ -124,7 +124,7 @@ def tile_block_pa_t_kernel(tc, x, attn_norm_w, W_q, W_k, W_v, out_0, out_1, out_
                 words = slice(half * 2 * P * 2, (half + 1) * 2 * P * 2)
                 dst = w_grouped_words[:, words].rearrange("p (f i u) -> p f i u", i=2, u=2)
                 src = w_flip[:].rearrange("p i u f -> p f i u")
-                copy(out=dst, in_=src)
+                copies[half](out=dst, in_=src)
 
         def quantise_weight(which):
             nc.vector.quantize_mx(
@@ -206,7 +206,7 @@ def tile_block_pa_t_kernel(tc, x, attn_norm_w, W_q, W_k, W_v, out_0, out_1, out_
                 stop=True,
             )
             by_head = acc[:].rearrange("p (n j) -> p n j", n=HEADS)
-            if bank < 6 or bank >= HALF_TILES and (bank % 5 in (0, 2, 3) if bank < LAST_NORM_BANK else bank % 2 == 0):
+            if bank < 7 or bank >= HALF_TILES and (bank % 9 in (0, 2, 4, 5, 7) if bank < LAST_NORM_BANK else bank % 2 == 0):
                 nc.scalar.copy(out=unit[:, :, g, :], in_=by_head)
             else:
                 nc.vector.tensor_copy(out=unit[:, :, g, :], in_=by_head)
@@ -217,7 +217,7 @@ def tile_block_pa_t_kernel(tc, x, attn_norm_w, W_q, W_k, W_v, out_0, out_1, out_
 
         due = {}
         for pair in range(HALF_PAIRS, PAIRS):
-            quant_bank = first_bank[pair - pair % HALF_PAIRS] - QUANT_LEAD + PAIR_SPACING * (pair % HALF_PAIRS)
+            quant_bank = first_bank[pair - pair % HALF_PAIRS] - QUANT_LEAD[pair * PAIR // BATCH_TILES] + PAIR_SPACING * (pair % HALF_PAIRS)
             for ahead, stage in (
                 (0, quantise),
                 (GAIN_AHEAD, apply_gain),
@@ -229,8 +229,8 @@ def tile_block_pa_t_kernel(tc, x, attn_norm_w, W_q, W_k, W_v, out_0, out_1, out_
 
         def results(bank):
             if bank == W_V_BANK:
-                transpose_weight(2, nc.vector.tensor_copy)
-            if bank == W_V_BANK + 2:
+                transpose_weight(2, (nc.scalar.copy, nc.vector.tensor_copy))
+            if bank == W_V_BANK + 3:
                 quantise_weight(2)
             for stage, pair in due.get(bank, []):
                 stage(pair)
@@ -255,7 +255,7 @@ def tile_block_pa_t_kernel(tc, x, attn_norm_w, W_q, W_k, W_v, out_0, out_1, out_
         keep_warm(8)
         sum_squares(0)
         scale_rows(0)
-        transpose_weight(0, nc.vector.tensor_copy)
+        transpose_weight(0, (nc.vector.tensor_copy, nc.vector.tensor_copy))
         sum_squares(1)
         scale_rows(1)
         keep_warm(2)
@@ -265,7 +265,7 @@ def tile_block_pa_t_kernel(tc, x, attn_norm_w, W_q, W_k, W_v, out_0, out_1, out_
         apply_gain(0)
         scale_rows(2)
         sum_squares(3)
-        transpose_weight(1, nc.scalar.copy)
+        transpose_weight(1, (nc.scalar.copy, nc.scalar.copy))
         quantise_weight(0)
         transpose_pair(1)
         keep_warm(2)

@@ -260,7 +260,7 @@ def tile_block_pa_t_kernel(tc, x, attn_norm_w, W_q, W_k, W_v, out_0, out_1, out_
         scale_rows(1)
         keep_warm(2)
         transpose_pair(0)
-        keep_warm(2)
+        keep_warm(1)
         sum_squares(2)
         apply_gain(0)
         scale_rows(2)
@@ -268,20 +268,18 @@ def tile_block_pa_t_kernel(tc, x, attn_norm_w, W_q, W_k, W_v, out_0, out_1, out_
         transpose_weight(1, (nc.scalar.copy, nc.scalar.copy))
         quantise_weight(0)
         transpose_pair(1)
-        keep_warm(2)
+        keep_warm(1)
         quantise(0)
         apply_gain(1)
         scale_rows(3)
         results(0)
         results(1)
         transpose_pair(2)
-        keep_warm(1)
         quantise(1)
         apply_gain(2)
         results(2)
         results(3)
         transpose_pair(3)
-        keep_warm(1)
         quantise(2)
         apply_gain(3)
         results(4)

@@ -80,7 +80,6 @@ def tile_block_pa_t_kernel(tc, x, attn_norm_w, W_q, W_k, W_v, out_0, out_1, out_
         x_codes = keep.tile([P, TOKEN_TILES * P], U32, align_bytes=64)
         x_scales = keep.tile([P, TOKEN_TILES * P], U8, align_bytes=64)
         sum_sq = keep.tile([P, TOKEN_TILES], F32)
-        rms = keep.tile([P, TOKEN_TILES], F32)
         inv_rms = keep.tile([P, TOKEN_TILES], F32)
         ident_f32 = keep.tile([P, P], F32)
         eps_col = keep.tile([P, 1], F32)
@@ -141,12 +140,10 @@ def tile_block_pa_t_kernel(tc, x, attn_norm_w, W_q, W_k, W_v, out_0, out_1, out_
                 )
             cols = slice(PAIR * pair, PAIR * (pair + 1))
             nc.scalar.activation(
-                out=rms[:, cols], in_=sum_sq[:, cols], func=FUNC.Sqrt, bias=eps_col[:], scale=1.0 / D
+                out=inv_rms[:, cols], in_=sum_sq[:, cols], func=FUNC.Abs_reciprocal_sqrt, bias=eps_col[:], scale=1.0 / D
             )
 
         def scale_rows(pair):
-            cols = slice(PAIR * pair, PAIR * (pair + 1))
-            nc.vector.reciprocal(out=inv_rms[:, cols], in_=rms[:, cols])
             x_over_rms = scaled_pool.tile([P, PAIR, PACK, P], F32)
             for h in range(PAIR):
                 i = PAIR * pair + h
@@ -242,7 +239,7 @@ def tile_block_pa_t_kernel(tc, x, attn_norm_w, W_q, W_k, W_v, out_0, out_1, out_
         nc.vector.memset(zeros[:], 0.0)
         make_identity(nc, ident_f32[:])
         nc.scalar.dma_start(out=gain_col[:], in_=attn_norm_w.rearrange("(p t) -> p t", t=PACK))
-        nc.scalar.activation(out=table_warm[:], in_=eps_col[:], func=FUNC.Sqrt)
+        nc.scalar.activation(out=table_warm[:], in_=eps_col[:], func=FUNC.Abs_reciprocal_sqrt)
         load_x(0, 0, PAIR)
         load_weight(0)
         for pair in range(1, HALF_PAIRS):

from contextlib import ExitStack

import concourse.mybir as mybir
from concourse.masks import make_identity

BF16 = mybir.dt.bfloat16
F32 = mybir.dt.float32
U32 = mybir.dt.uint32
U8 = mybir.dt.uint8
FP8X4 = mybir.dt.float8_e4m3fn_x4
MULT = mybir.AluOpType.mult
FUNC = mybir.ActivationFunctionType

P = 128
PACK = 4
D = P * PACK
BATCH = 2
SEQ = 2048
HEADS = 8
HEAD_DIM = D // HEADS
EPS = 1e-6
PROJECTIONS = 3

BATCH_TILES = SEQ // P
HALF_TILES = BATCH_TILES // 2
TOKEN_TILES = BATCH * BATCH_TILES

PAIR = 2
PAIRS = TOKEN_TILES // PAIR
HALF_PAIRS = HALF_TILES // PAIR
BANKS = TOKEN_TILES * PROJECTIONS
ACC_BANKS = 5

QUANT_LEAD = (8, 7)
PAIR_SPACING = 4
SQUARES_AHEAD = 12
SCALE_AHEAD = 8
TRANSPOSE_AHEAD = 3
GAIN_AHEAD = 2
LAST_NORM_BANK = 68
W_V_BANK = 6

FLOPS = 2 * BATCH * SEQ * D * PROJECTIONS * D


def tile_block_pa_t_kernel(tc, x, attn_norm_w, W_q, W_k, W_v, out_0, out_1, out_2):
    nc = tc.nc
    weights = (W_q, W_k, W_v)
    outs = (out_0, out_1, out_2)
    x_by_partition = x.rearrange("b (p g) d -> b p g d", g=BATCH_TILES)

    quarter = HALF_TILES // 2
    stores = [(0, which, first, quarter) for which in (0, 1) for first in (0, quarter)] + [(0, 2, 0, HALF_TILES)]
    stores += [(0, which, HALF_TILES, HALF_TILES) for which in range(PROJECTIONS)]
    stores += [(1, which, first, HALF_TILES) for first in (0, HALF_TILES) for which in (0, 1)]
    stores += [(1, 2, 0, BATCH_TILES)]
    banks = []
    for store in stores:
        batch, which, first, tiles = store
        for g in range(first, first + tiles):
            banks.append((batch, which, g, store if g == first + tiles - 1 else None))
    first_bank = {}
    for n, (batch, which, g, store) in enumerate(banks):
        first_bank.setdefault((batch * BATCH_TILES + g) // PAIR, n)

    with ExitStack() as stack:
        keep = stack.enter_context(tc.tile_pool(name="keep", bufs=1))
        junk_pool = stack.enter_context(tc.tile_pool(name="junk", bufs=2))
        scaled_pool = stack.enter_context(tc.tile_pool(name="scaled", bufs=3))
        normed_pool = stack.enter_context(tc.tile_pool(name="normed", bufs=2))
        w_grouped_pool = stack.enter_context(tc.tile_pool(name="w_grouped", bufs=2))
        unit_pool = stack.enter_context(tc.tile_pool(name="unit", bufs=4))
        flip_pool = stack.enter_context(tc.psum_pool(name="flip", bufs=3))
        acc_pool = stack.enter_context(tc.psum_pool(name="acc", bufs=ACC_BANKS))

        x_sb = keep.tile([P, TOKEN_TILES, D], BF16)
        w_sb = keep.tile([P, PROJECTIONS, 2, 2, D], BF16)
        w_codes = keep.tile([P, PROJECTIONS, D], U32, align_bytes=64)
        w_scales = keep.tile([P, PROJECTIONS, D], U8, align_bytes=64)
        x_codes = keep.tile([P, TOKEN_TILES * P], U32, align_bytes=64)
        x_scales = keep.tile([P, TOKEN_TILES * P], U8, align_bytes=64)
        sum_sq = keep.tile([P, TOKEN_TILES], F32)
        inv_rms = keep.tile([P, TOKEN_TILES], F32)
        ident_f32 = keep.tile([P, P], F32)
        eps_col = keep.tile([P, 1], F32)
        table_warm = keep.tile([P, 1], F32)
        zeros = keep.tile([P, D], BF16)
        gain_col = keep.tile([P, PACK], BF16)

        grouped = {}
        scaled = {}
        flipped = {}
        normed = {}
        units = {}

        def keep_warm(count):
            nothing = acc_pool.tile([P, D], F32, tag="acc")
            for i in range(count):
                nc.tensor.matmul(nothing[:], lhsT=zeros[:, 0:P], rhs=zeros[:], start=True, stop=True)

        def load_x(batch, first, tiles):
            start = batch * BATCH_TILES + first
            nc.sync.dma_start(
                out=x_sb[:, start : start + tiles, :], in_=x_by_partition[batch, :, first : first + tiles, :]
            )

        def load_weight(which):
            nc.sync.dma_start(
                out=w_sb[:, which, :, :, :],
                in_=weights[which].rearrange("(h p i) k -> p h i k", h=2, i=2),
            )

        def transpose_weight(which, copies):
            w_grouped = w_grouped_pool.tile([P, D, PACK], BF16, align_bytes=64)
            grouped[which] = w_grouped
            w_grouped_words = w_grouped[:].rearrange("p f t -> p (f t)").bitcast(F32)
            for half in range(2):
                w_flip = acc_pool.tile([P, 2, 2, P], F32, tag="acc")
                for i in range(2):
                    w_words = w_sb[:, which, half, i, :].bitcast(F32)
                    for u in range(2):
                        nc.tensor.transpose(w_flip[:, i, u, :], w_words[:, u::2], ident_f32[:])
                words = slice(half * 2 * P * 2, (half + 1) * 2 * P * 2)
                dst = w_grouped_words[:, words].rearrange("p (f i u) -> p f i u", i=2, u=2)
                src = w_flip[:].rearrange("p i u f -> p f i u")
                copies[half](out=dst, in_=src)

        def quantise_weight(which):
            nc.vector.quantize_mx(
                out=w_codes[:, which, :].bitcast(FP8X4),
                scales=w_scales[:, which, :],
                in_=grouped[which][:].rearrange("p f t -> p (f t)"),
            )

        def sum_squares(pair):
            for i in range(PAIR * pair, PAIR * (pair + 1)):
                squares = junk_pool.tile([P, D], BF16)
                nc.scalar.activation(
                    out=squares[:], in_=x_sb[:, i, :], func=FUNC.Square, accum_out=sum_sq[:, i : i + 1]
                )
            cols = slice(PAIR * pair, PAIR * (pair + 1))
            nc.scalar.activation(
                out=inv_rms[:, cols], in_=sum_sq[:, cols], func=FUNC.Abs_reciprocal_sqrt, bias=eps_col[:], scale=1.0 / D
            )

        def scale_rows(pair):
            x_over_rms = scaled_pool.tile([P, PAIR, PACK, P], F32)
            for h in range(PAIR):
                i = PAIR * pair + h
                nc.gpsimd.tensor_scalar(
                    out=x_over_rms[:, h, :, :],
                    in0=x_sb[:, i, :].rearrange("l (q t) -> l t q", t=PACK),
                    scalar1=inv_rms[:, i : i + 1],
                    scalar2=1.0,
                    op0=MULT,
                    op1=MULT,
                )
            scaled[pair] = x_over_rms

        def transpose_pair(pair):
            x_flips = []
            for h in range(PAIR):
                x_flip = flip_pool.tile([P, PACK, P], F32, tag="flip")
                for t in range(PACK):
                    nc.tensor.transpose(x_flip[:, t, :], scaled[pair][:, h, t, :], ident_f32[:])
                x_flips.append(x_flip)
            flipped[pair] = x_flips

        def apply_gain(pair):
            xn = normed_pool.tile([P, PAIR, P, PACK], BF16, align_bytes=64)
            for h in range(PAIR):
                nc.vector.tensor_tensor(
                    out=xn[:, h, :, :],
                    in0=flipped[pair][h][:].rearrange("p t l -> p l t"),
                    in1=gain_col[:].unsqueeze(1).to_broadcast([P, P, PACK]),
                    op=MULT,
                )
            normed[pair] = xn

        def quantise(pair):
            cols = slice(pair * PAIR * P, (pair + 1) * PAIR * P)
            nc.vector.quantize_mx(
                out=x_codes[:, cols].bitcast(FP8X4),
                scales=x_scales[:, cols],
                in_=normed[pair][:].rearrange("p h l t -> p (h l t)"),
            )

        def project(bank):
            batch, which, g, store = banks[bank]
            if (batch, which) not in units:
                new_unit = unit_pool.tile([P, HEADS, BATCH_TILES, HEAD_DIM], F32)
                units[(batch, which)] = new_unit
            unit = units[(batch, which)]
            cols = slice((batch * BATCH_TILES + g) * P, (batch * BATCH_TILES + g + 1) * P)
            acc = acc_pool.tile([P, D], F32, tag="acc")
            nc.tensor.matmul_mx(
                out=acc[:],
                lhsT=x_codes[:, cols].bitcast(FP8X4),
                lhsT_scale=x_scales[:, cols],
                rhs=w_codes[:, which, :].bitcast(FP8X4),
                rhs_scale=w_scales[:, which, :],
                start=True,
                stop=True,
            )
            by_head = acc[:].rearrange("p (n j) -> p n j", n=HEADS)
            if bank < 7 or bank >= HALF_TILES and (bank % 9 in (0, 2, 4, 5, 7) if bank < LAST_NORM_BANK else bank % 2 == 0):
                nc.scalar.copy(out=unit[:, :, g, :], in_=by_head)
            else:
                nc.vector.tensor_copy(out=unit[:, :, g, :], in_=by_head)
            if store is not None:
                tiles = slice(store[2], store[2] + store[3])
                by_partition = outs[which][batch, :, :, :].rearrange("n (p g) j -> p n g j", g=BATCH_TILES)
                nc.sync.dma_start(out=by_partition[:, :, tiles, :], in_=unit[:, :, tiles, :])

        due = {}
        for pair in range(HALF_PAIRS, PAIRS):
            quant_bank = first_bank[pair - pair % HALF_PAIRS] - QUANT_LEAD[pair * PAIR // BATCH_TILES] + PAIR_SPACING * (pair % HALF_PAIRS)
            for ahead, stage in (
                (0, quantise),
                (GAIN_AHEAD, apply_gain),
                (TRANSPOSE_AHEAD, transpose_pair),
                (SCALE_AHEAD, scale_rows),
                (SQUARES_AHEAD, sum_squares),
            ):
                due.setdefault(quant_bank - ahead, []).append((stage, pair))

        def results(bank):
            if bank == W_V_BANK:
                transpose_weight(2, (nc.scalar.copy, nc.vector.tensor_copy))
            if bank == W_V_BANK + 3:
                quantise_weight(2)
            for stage, pair in due.get(bank, []):
                stage(pair)
            project(bank)

        stack.enter_context(tc.manual_schedule())

        nc.vector.memset(eps_col[:], EPS)
        nc.vector.memset(zeros[:], 0.0)
        make_identity(nc, ident_f32[:])
        nc.scalar.dma_start(out=gain_col[:], in_=attn_norm_w.rearrange("(p t) -> p t", t=PACK))
        nc.scalar.activation(out=table_warm[:], in_=eps_col[:], func=FUNC.Abs_reciprocal_sqrt)
        load_x(0, 0, PAIR)
        load_weight(0)
        for pair in range(1, HALF_PAIRS):
            load_x(0, PAIR * pair, PAIR)
        load_weight(1)
        load_x(0, HALF_TILES, HALF_TILES)
        load_weight(2)
        load_x(1, 0, BATCH_TILES)

        keep_warm(8)
        sum_squares(0)
        scale_rows(0)
        transpose_weight(0, (nc.vector.tensor_copy, nc.vector.tensor_copy))
        sum_squares(1)
        scale_rows(1)
        keep_warm(2)
        transpose_pair(0)
        keep_warm(1)
        sum_squares(2)
        apply_gain(0)
        scale_rows(2)
        sum_squares(3)
        transpose_weight(1, (nc.scalar.copy, nc.scalar.copy))
        quantise_weight(0)
        transpose_pair(1)
        keep_warm(1)
        quantise(0)
        apply_gain(1)
        scale_rows(3)
        results(0)
        results(1)
        transpose_pair(2)
        quantise(1)
        apply_gain(2)
        results(2)
        results(3)
        transpose_pair(3)
        quantise(2)
        apply_gain(3)
        results(4)
        results(5)
        quantise(3)
        quantise_weight(1)

        for bank in range(6, BANKS):
            results(bank)
